import numpy as np
import ml_dtypes


def mxq(x, axis, fmt="e4m3"):
    dtype, down = {"e4m3": (ml_dtypes.float8_e4m3fn, 7), "e5m2": (ml_dtypes.float8_e5m2, 14)}[fmt]
    v = np.moveaxis(np.asarray(x, np.float32).astype(ml_dtypes.bfloat16).astype(np.float64), axis, -1)
    blocks = v.reshape(v.shape[:-1] + (-1, 32))
    amax = np.abs(blocks).max(-1, keepdims=True)
    byte = np.maximum(np.where(amax > 0, np.frexp(amax)[1] - 1 + 127, 0) - down, 1)
    scale = np.exp2(byte - 127.0)
    codes = (blocks / scale).astype(np.float32).astype(dtype).astype(np.float64)
    return np.moveaxis((codes * scale).reshape(v.shape), -1, axis)


WIDE = False


def mx_kscale(k):
    if not WIDE:
        return np.ones(k)
    levels = np.array([10, -10, 5, -5, 0])
    a = np.random.permutation(np.resize(levels, k // 512 * 4)).reshape(k // 512, 4)
    idx = np.arange(k)
    return np.exp2(a[idx // 512, idx % 128 // 32])


BF16 = ml_dtypes.bfloat16


def bf(x):
    return np.asarray(x, np.float32).astype(BF16)


def f64(x):
    return np.asarray(x).astype(np.float64)


L, B, P, H, DH, DM = 2, 8, 513, 8, 64, 512
M = L + 1
K = L * H * DH
R = P - 1
THR = 0.001


def sg(v):
    return v


def setup_inputs():
    s = mx_kscale(K).reshape(L, H, DH)
    return {
        "attn_cache": bf(np.random.standard_normal((L, B, P, H, DH)) * s[:, None, None]),
        "mlp_cache": bf(np.random.standard_normal((M, B, P, DM)) / np.sqrt(M)),
        "mlp_mask": bf(np.random.uniform(0.0, 1.0, (B, M))),
        "attn_mask": bf(np.random.uniform(0.0, 1.0, (B, L, H))),
        "modal_attention": bf(np.random.standard_normal((L, H, DH)) * s),
        "modal_mlp": bf(np.random.standard_normal((M, DM)) / np.sqrt(M)),
        "W_O": bf(np.random.standard_normal((L, H, DH, DM)) * 2.0 / np.sqrt(K) / s[..., None]),
        "post_bias": bf(np.random.standard_normal((L, DM)) * 0.3 / np.sqrt(L)),
        "orig_in": bf(np.random.standard_normal((B, P, DM))),
    }


def reference(attn_cache, mlp_cache, mlp_mask, attn_mask, modal_attention, modal_mlp, W_O, post_bias, orig_in):
    modal_attention = f64(modal_attention)
    modal_mlp = f64(modal_mlp)
    mm = f64(mlp_mask)[:, None, :, None]
    mlp_stack = np.moveaxis(f64(mlp_cache), 0, 2)
    out = (mm * mlp_stack).sum(axis=2)
    mlp_blend = np.where(mm < THR, (1.0 - mm) * modal_mlp, (1.0 - mm) * sg(modal_mlp))
    out = out + mlp_blend.sum(axis=2)
    am = f64(attn_mask)[:, None, :, :, None]
    attn_stack = np.moveaxis(f64(attn_cache), 0, 2)
    attn_blend = np.where(am < THR, (1.0 - am) * modal_attention, (1.0 - am) * sg(modal_attention))
    attn_term = am * attn_stack + attn_blend
    attn_term = attn_term[:, 1:].reshape(B, R, K)
    attn_term = mxq(attn_term, 2, "e4m3") @ mxq(f64(W_O).reshape(K, DM), 0, "e4m3")
    out = out[:, 1:] + attn_term + f64(post_bias).sum(axis=0)
    return np.concatenate([sg(f64(orig_in)[:, :1]), out], axis=1)

@@ -1,0 +1,203 @@
+from contextlib import ExitStack
+
+import concourse.bass as bass
+import concourse.mybir as mybir
+import concourse.tile as tile
+from concourse.masks import make_identity
+
+F32 = mybir.dt.float32
+BF16 = mybir.dt.bfloat16
+U32 = mybir.dt.uint32
+U8 = mybir.dt.uint8
+FP8X4 = mybir.dt.float8_e4m3fn_x4
+ALU = mybir.AluOpType
+ACT = mybir.ActivationFunctionType
+
+L, B, POS, H, DH, DM = 2, 8, 513, 8, 64, 512
+M = 3
+P = 128
+J = 4
+R = POS - 1
+KL = H * DH
+
+FLOPS = 2 * B * R * L * KL * DM
+BYTES = 2 * (L * B * R * KL + M * B * R * DM + L * KL * DM) + 4 * B * POS * DM
+
+V_INTERLEAVE = ()
+
+
+def interleave(eng_copy, dst, src):
+    eng_copy(
+        out=dst.rearrange("p (c i) t -> p c t i", i=4),
+        in_=src.rearrange("p t (c i) -> p c t i", i=4),
+    )
+
+
+def tile_edgepruner_t_kernel(
+    tc, attn_cache, mlp_cache, mlp_mask, attn_mask, modal_attention, modal_mlp, W_O, post_bias, orig_in, out
+):
+    nc = tc.nc
+    with ExitStack() as ctx:
+        const = ctx.enter_context(tc.tile_pool(name="const", bufs=1))
+        apool = ctx.enter_context(tc.tile_pool(name="apool", bufs=3))
+        mpool = ctx.enter_context(tc.tile_pool(name="mpool", bufs=3))
+        opool = ctx.enter_context(tc.tile_pool(name="opool", bufs=3))
+        ppool = ctx.enter_context(tc.tile_pool(name="ppool", bufs=3))
+        gpool = ctx.enter_context(tc.tile_pool(name="gpool", bufs=3))
+        cpool = ctx.enter_context(tc.tile_pool(name="cpool", bufs=4))
+        psT = ctx.enter_context(tc.psum_pool(name="psT", bufs=4))
+        psO = ctx.enter_context(tc.psum_pool(name="psO", bufs=4))
+
+        wraw = const.tile([P, 2 * L, 2, DM], BF16)
+        nc.sync.dma_start(
+            out=wraw[:].rearrange("p g e n -> p g (e n)"),
+            in_=W_O.rearrange("l h d n -> (l h d) n").rearrange("(g p e) n -> p g (e n)", g=2 * L, p=P, e=2),
+        )
+        am_bc = const.tile([P, B * L * H], BF16)
+        nc.scalar.dma_start(out=am_bc[:], in_=attn_mask.rearrange("b l h -> (b l h)").partition_broadcast(P))
+        modalT = const.tile([P, 2 * L, 2], BF16)
+        with nc.allow_non_contiguous_dma(reason="512 four-byte pieces, once"):
+            nc.scalar.dma_start(
+                out=modalT[:],
+                in_=modal_attention.rearrange("l h d -> (l h d)").rearrange("(g p e) -> p g e", g=2 * L, p=P, e=2),
+            )
+        mm_bc = const.tile([P, B * M], BF16)
+        nc.scalar.dma_start(out=mm_bc[:], in_=mlp_mask.rearrange("b m -> (b m)").partition_broadcast(P))
+        mmr = const.tile([B, M], BF16)
+        nc.scalar.dma_start(out=mmr[:], in_=mlp_mask)
+        mod8 = const.tile([B, M, DM], BF16)
+        nc.scalar.dma_start(
+            out=mod8[:].rearrange("b m n -> b (m n)"), in_=modal_mlp.rearrange("m n -> (m n)").partition_broadcast(B)
+        )
+        pb8 = const.tile([B, L, DM], BF16)
+        nc.scalar.dma_start(
+            out=pb8[:].rearrange("b l n -> b (l n)"), in_=post_bias.rearrange("l n -> (l n)").partition_broadcast(B)
+        )
+        o8 = const.tile([B, DM], BF16)
+        nc.scalar.dma_start(out=o8[:], in_=orig_in[:, 0, :])
+
+        ident = const.tile([P, P], F32)
+        make_identity(nc, ident[:])
+
+        scl = const.tile([P, B, L, 2], F32)
+        amv = am_bc[:].rearrange("p (b l u g) -> p b l u g", b=B, l=L, u=2, g=4)
+        for g in range(4):
+            nc.vector.tensor_copy(out=scl[32 * g : 32 * g + 32], in_=amv[32 * g : 32 * g + 32, :, :, :, g])
+        om = const.tile([P, B * L * 2], F32)
+        nc.vector.tensor_scalar(
+            out=om[:], in0=scl[:].rearrange("p b l u -> p (b l u)"), scalar1=-1.0, scalar2=1.0, op0=ALU.mult, op1=ALU.add
+        )
+        bia = const.tile([P, B, 2 * L, 2], F32)
+        nc.vector.tensor_tensor(
+            out=bia[:],
+            in0=om[:].rearrange("p (b g) -> p b g", g=2 * L).unsqueeze(3).to_broadcast([P, B, 2 * L, 2]),
+            in1=modalT[:].unsqueeze(1).to_broadcast([P, B, 2 * L, 2]),
+            op=ALU.mult,
+        )
+        mmf = const.tile([P, B * M], F32)
+        nc.vector.tensor_copy(out=mmf[:], in_=mm_bc[:])
+
+        crow = const.tile([P, DM], F32)
+        nc.vector.memset(crow[:], 0.0)
+        omr = const.tile([B, M], F32)
+        nc.vector.tensor_scalar(out=omr[:], in0=mmr[:], scalar1=-1.0, scalar2=1.0, op0=ALU.mult, op1=ALU.add)
+        nc.vector.tensor_tensor(out=crow[0:B, :], in0=pb8[:, 0, :], in1=pb8[:, 1, :], op=ALU.add)
+        for m in range(M):
+            nc.vector.scalar_tensor_tensor(
+                out=crow[0:B, :], in0=mod8[:, m, :], scalar=omr[:, m : m + 1], in1=crow[0:B, :], op0=ALU.mult, op1=ALU.add
+            )
+        cbc = const.tile([P, B, DM], F32)
+        for b in range(B):
+            po = psO.tile([P, DM], F32)
+            nc.tensor.matmul(out=po[:], lhsT=ident[:, b : b + 1].to_broadcast([P, P]), rhs=crow[:], start=True, stop=True)
+            nc.scalar.copy(out=cbc[:, b, :], in_=po[:])
+
+        o8f = const.tile([B, DM], F32)
+        nc.vector.tensor_copy(out=o8f[:], in_=o8[:])
+        nc.scalar.dma_start(out=out[:, 0, :], in_=o8f[:])
+
+        wg = const.tile([P, L, DM, 4], BF16, align_bytes=64)
+        wc = const.tile([P, L, DM], U32, align_bytes=64)
+        ws = const.tile([P, L, DM], U8, align_bytes=64)
+        for l in range(L):
+            interleave(nc.vector.tensor_copy, wg[:, l], wraw[:, 2 * l : 2 * l + 2].rearrange("p u e n -> p (u e) n"))
+        for l in range(L):
+            nc.vector.quantize_mx(
+                out=wc[:, l, :].bitcast(FP8X4), scales=ws[:, l, :], in_=wg[:, l].rearrange("p n t -> p (n t)")
+            )
+
+        for b in range(B):
+            xa = apool.tile([P, L, J, KL], BF16)
+            nc.sync.dma_start(
+                out=xa[:].rearrange("p l j k -> p l (j k)"),
+                in_=attn_cache[:, b, 1:POS, :, :].rearrange("l (p j) h d -> p l (j h d)", j=J),
+            )
+            xm = mpool.tile([P, M, J, DM], BF16)
+            nc.sync.dma_start(
+                out=xm[:].rearrange("p m j n -> p m (j n)"),
+                in_=mlp_cache[:, b, 1:POS, :].rearrange("m (p j) n -> p m (j n)", j=J),
+            )
+
+            codes = []
+            for l in range(L):
+                planes = ppool.tile([P, 4, J * P], BF16)
+                for u in range(2):
+                    pt = psT.tile([P, J, P], F32)
+                    for j in range(J):
+                        nc.tensor.transpose(
+                            out=pt[:, j, :], in_=xa[:, l, j, :].bitcast(F32)[:, P * u : P * u + P], identity=ident[:]
+                        )
+                    ptv = pt[:].rearrange("p j r -> p (j r)").bitcast(BF16).rearrange("p (c e) -> p c e", e=2)
+                    for e in range(2):
+                        nc.scalar.activation(
+                            out=planes[:, 2 * u + e, :],
+                            in_=ptv[:, :, e],
+                            func=ACT.Identity,
+                            bias=bia[:, b, 2 * l + u, e : e + 1],
+                            scale=scl[:, b, l, u : u + 1],
+                        )
+                grp = gpool.tile([P, J * P, 4], BF16, align_bytes=64)
+                if (b, l) in V_INTERLEAVE:
+                    interleave(nc.vector.tensor_copy, grp[:], planes[:])
+                else:
+                    interleave(nc.scalar.copy, grp[:], planes[:])
+                ac = cpool.tile([P, J * P], U32, align_bytes=64)
+                asc = cpool.tile([P, J * P], U8, align_bytes=64)
+                nc.vector.quantize_mx(out=ac[:].bitcast(FP8X4), scales=asc[:], in_=grp[:].rearrange("p c t -> p (c t)"))
+                codes.append((ac, asc))
+
+            acc = opool.tile([P, J, DM], F32)
+            nc.vector.scalar_tensor_tensor(
+                out=acc[:],
+                in0=xm[:, 0],
+                scalar=mmf[:, M * b : M * b + 1],
+                in1=cbc[:, b, :].unsqueeze(1).to_broadcast([P, J, DM]),
+                op0=ALU.mult,
+                op1=ALU.add,
+            )
+            for m in range(1, M):
+                nc.vector.scalar_tensor_tensor(
+                    out=acc[:],
+                    in0=xm[:, m],
+                    scalar=mmf[:, M * b + m : M * b + m + 1],
+                    in1=acc[:],
+                    op0=ALU.mult,
+                    op1=ALU.add,
+                )
+            for j in range(J):
+                po = psO.tile([P, DM], F32)
+                for l in range(L):
+                    ac, asc = codes[l]
+                    nc.tensor.matmul_mx(
+                        out=po[:],
+                        lhsT=ac[:, P * j : P * j + P].bitcast(FP8X4),
+                        lhsT_scale=asc[:, P * j : P * j + P],
+                        rhs=wc[:, l, :].bitcast(FP8X4),
+                        rhs_scale=ws[:, l, :],
+                        start=(l == 0),
+                        stop=(l == L - 1),
+                    )
+                nc.vector.tensor_tensor(out=acc[:, j, :], in0=acc[:, j, :], in1=po[:], op=ALU.add)
+            nc.sync.dma_start(
+                out=out[b, 1:POS, :].rearrange("(p j) n -> p (j n)", j=J), in_=acc[:].rearrange("p j n -> p (j n)")
+            )

@@ -1,8 +1,6 @@
 from contextlib import ExitStack
 
-import concourse.bass as bass
 import concourse.mybir as mybir
-import concourse.tile as tile
 from concourse.masks import make_identity
 
 F32 = mybir.dt.float32
@@ -23,6 +21,7 @@ KL = H * DH
 FLOPS = 2 * B * R * L * KL * DM
 BYTES = 2 * (L * B * R * KL + M * B * R * DM + L * KL * DM) + 4 * B * POS * DM
 
+PIN = False
 V_INTERLEAVE = ()
 
 
@@ -39,20 +38,49 @@ def tile_edgepruner_t_kernel(
     nc = tc.nc
     with ExitStack() as ctx:
         const = ctx.enter_context(tc.tile_pool(name="const", bufs=1))
-        apool = ctx.enter_context(tc.tile_pool(name="apool", bufs=3))
-        mpool = ctx.enter_context(tc.tile_pool(name="mpool", bufs=3))
+        apool = ctx.enter_context(tc.tile_pool(name="apool", bufs=4))
+        mpool = ctx.enter_context(tc.tile_pool(name="mpool", bufs=4))
         opool = ctx.enter_context(tc.tile_pool(name="opool", bufs=3))
         ppool = ctx.enter_context(tc.tile_pool(name="ppool", bufs=3))
         gpool = ctx.enter_context(tc.tile_pool(name="gpool", bufs=3))
         cpool = ctx.enter_context(tc.tile_pool(name="cpool", bufs=4))
         psT = ctx.enter_context(tc.psum_pool(name="psT", bufs=4))
         psO = ctx.enter_context(tc.psum_pool(name="psO", bufs=4))
+        if PIN:
+            ctx.enter_context(tc.manual_schedule())
+
+        xas = {}
+        xms = {}
+
+        def load_attn(b, fine):
+            xa = apool.tile([P, L, J, KL], BF16, name="xa")
+            xas[b] = xa
+            src = attn_cache[:, b, 1:POS, :, :].rearrange("l (p j) h d -> p l (j h d)", j=J)
+            dst = xa[:].rearrange("p l j k -> p l (j k)")
+            if fine:
+                return [(dst[:, l, :], src[:, l, :]) for l in range(L)]
+            return [(dst, src)]
+
+        def load_mlp(b, fine):
+            xm = mpool.tile([P, M, J, DM], BF16, name="xm")
+            xms[b] = xm
+            src = mlp_cache[:, b, 1:POS, :].rearrange("m (p j) n -> p m (j n)", j=J)
+            dst = xm[:].rearrange("p m j n -> p m (j n)")
+            if fine:
+                return [(dst[:, m, :], src[:, m, :]) for m in range(M)]
+            return [(dst, src)]
+
+        def issue(pairs):
+            for dst, src in pairs:
+                nc.sync.dma_start(out=dst, in_=src)
 
         wraw = const.tile([P, 2 * L, 2, DM], BF16)
-        nc.sync.dma_start(
-            out=wraw[:].rearrange("p g e n -> p g (e n)"),
-            in_=W_O.rearrange("l h d n -> (l h d) n").rearrange("(g p e) n -> p g (e n)", g=2 * L, p=P, e=2),
-        )
+        wsrc = W_O.rearrange("l h d n -> (l h d) n").rearrange("(g p e) n -> p g (e n)", g=2 * L, p=P, e=2)
+        wdst = wraw[:].rearrange("p g e n -> p g (e n)")
+        a0 = load_attn(0, True)
+        m0 = load_mlp(0, True)
+        issue([(wdst[:, 0:2, :], wsrc[:, 0:2, :]), a0[0], (wdst[:, 2:4, :], wsrc[:, 2:4, :]), m0[0], a0[1], m0[1], m0[2]])
+
         am_bc = const.tile([P, B * L * H], BF16)
         nc.scalar.dma_start(out=am_bc[:], in_=attn_mask.rearrange("b l h -> (b l h)").partition_broadcast(P))
         modalT = const.tile([P, 2 * L, 2], BF16)
@@ -61,8 +89,6 @@ def tile_edgepruner_t_kernel(
                 out=modalT[:],
                 in_=modal_attention.rearrange("l h d -> (l h d)").rearrange("(g p e) -> p g e", g=2 * L, p=P, e=2),
             )
-        mm_bc = const.tile([P, B * M], BF16)
-        nc.scalar.dma_start(out=mm_bc[:], in_=mlp_mask.rearrange("b m -> (b m)").partition_broadcast(P))
         mmr = const.tile([B, M], BF16)
         nc.scalar.dma_start(out=mmr[:], in_=mlp_mask)
         mod8 = const.tile([B, M, DM], BF16)
@@ -73,12 +99,20 @@ def tile_edgepruner_t_kernel(
         nc.scalar.dma_start(
             out=pb8[:].rearrange("b l n -> b (l n)"), in_=post_bias.rearrange("l n -> (l n)").partition_broadcast(B)
         )
+        mm_bc = const.tile([P, B * M], BF16)
+        nc.scalar.dma_start(out=mm_bc[:], in_=mlp_mask.rearrange("b m -> (b m)").partition_broadcast(P))
         o8 = const.tile([B, DM], BF16)
         nc.scalar.dma_start(out=o8[:], in_=orig_in[:, 0, :])
 
         ident = const.tile([P, P], F32)
         make_identity(nc, ident[:])
 
+        for b in range(1, min(4, 4)):
+            issue(load_attn(b, False))
+            issue(load_mlp(b, False))
+
+        crow = const.tile([P, DM], F32)
+        nc.vector.memset(crow[:], 0.0)
         scl = const.tile([P, B, L, 2], F32)
         amv = am_bc[:].rearrange("p (b l u g) -> p b l u g", b=B, l=L, u=2, g=4)
         for g in range(4):
@@ -94,11 +128,6 @@ def tile_edgepruner_t_kernel(
             in1=modalT[:].unsqueeze(1).to_broadcast([P, B, 2 * L, 2]),
             op=ALU.mult,
         )
-        mmf = const.tile([P, B * M], F32)
-        nc.vector.tensor_copy(out=mmf[:], in_=mm_bc[:])
-
-        crow = const.tile([P, DM], F32)
-        nc.vector.memset(crow[:], 0.0)
         omr = const.tile([B, M], F32)
         nc.vector.tensor_scalar(out=omr[:], in0=mmr[:], scalar1=-1.0, scalar2=1.0, op0=ALU.mult, op1=ALU.add)
         nc.vector.tensor_tensor(out=crow[0:B, :], in0=pb8[:, 0, :], in1=pb8[:, 1, :], op=ALU.add)
@@ -106,88 +135,88 @@ def tile_edgepruner_t_kernel(
             nc.vector.scalar_tensor_tensor(
                 out=crow[0:B, :], in0=mod8[:, m, :], scalar=omr[:, m : m + 1], in1=crow[0:B, :], op0=ALU.mult, op1=ALU.add
             )
+        mmf = const.tile([P, B * M], F32)
+        nc.vector.tensor_copy(out=mmf[:], in_=mm_bc[:])
+
         cbc = const.tile([P, B, DM], F32)
-        for b in range(B):
-            po = psO.tile([P, DM], F32)
+
+        def spread_const(b):
+            po = psO.tile([P, DM], F32, name="po")
             nc.tensor.matmul(out=po[:], lhsT=ident[:, b : b + 1].to_broadcast([P, P]), rhs=crow[:], start=True, stop=True)
             nc.scalar.copy(out=cbc[:, b, :], in_=po[:])
-
-        o8f = const.tile([B, DM], F32)
-        nc.vector.tensor_copy(out=o8f[:], in_=o8[:])
-        nc.scalar.dma_start(out=out[:, 0, :], in_=o8f[:])
 
         wg = const.tile([P, L, DM, 4], BF16, align_bytes=64)
         wc = const.tile([P, L, DM], U32, align_bytes=64)
         ws = const.tile([P, L, DM], U8, align_bytes=64)
-        for l in range(L):
-            interleave(nc.vector.tensor_copy, wg[:, l], wraw[:, 2 * l : 2 * l + 2].rearrange("p u e n -> p (u e) n"))
-        for l in range(L):
+
+        def w_regroup(l, eng_copy):
+            interleave(eng_copy, wg[:, l], wraw[:, 2 * l : 2 * l + 2].rearrange("p u e n -> p (u e) n"))
+
+        def w_quant(l):
             nc.vector.quantize_mx(
                 out=wc[:, l, :].bitcast(FP8X4), scales=ws[:, l, :], in_=wg[:, l].rearrange("p n t -> p (n t)")
             )
 
-        for b in range(B):
-            xa = apool.tile([P, L, J, KL], BF16)
-            nc.sync.dma_start(
-                out=xa[:].rearrange("p l j k -> p l (j k)"),
-                in_=attn_cache[:, b, 1:POS, :, :].rearrange("l (p j) h d -> p l (j h d)", j=J),
-            )
-            xm = mpool.tile([P, M, J, DM], BF16)
-            nc.sync.dma_start(
-                out=xm[:].rearrange("p m j n -> p m (j n)"),
-                in_=mlp_cache[:, b, 1:POS, :].rearrange("m (p j) n -> p m (j n)", j=J),
-            )
+        codes = {}
+        accs = {}
 
-            codes = []
-            for l in range(L):
-                planes = ppool.tile([P, 4, J * P], BF16)
-                for u in range(2):
-                    pt = psT.tile([P, J, P], F32)
-                    for j in range(J):
-                        nc.tensor.transpose(
-                            out=pt[:, j, :], in_=xa[:, l, j, :].bitcast(F32)[:, P * u : P * u + P], identity=ident[:]
-                        )
-                    ptv = pt[:].rearrange("p j r -> p (j r)").bitcast(BF16).rearrange("p (c e) -> p c e", e=2)
-                    for e in range(2):
-                        nc.scalar.activation(
-                            out=planes[:, 2 * u + e, :],
-                            in_=ptv[:, :, e],
-                            func=ACT.Identity,
-                            bias=bia[:, b, 2 * l + u, e : e + 1],
-                            scale=scl[:, b, l, u : u + 1],
-                        )
-                grp = gpool.tile([P, J * P, 4], BF16, align_bytes=64)
-                if (b, l) in V_INTERLEAVE:
-                    interleave(nc.vector.tensor_copy, grp[:], planes[:])
-                else:
-                    interleave(nc.scalar.copy, grp[:], planes[:])
-                ac = cpool.tile([P, J * P], U32, align_bytes=64)
-                asc = cpool.tile([P, J * P], U8, align_bytes=64)
-                nc.vector.quantize_mx(out=ac[:].bitcast(FP8X4), scales=asc[:], in_=grp[:].rearrange("p c t -> p (c t)"))
-                codes.append((ac, asc))
+        def t1(b, l):
+            xa = xas[b]
+            planes = ppool.tile([P, 4, J * P], BF16, name="planes")
+            for u in range(2):
+                pt = psT.tile([P, J, P], F32, name="pt")
+                for j in range(J):
+                    nc.tensor.transpose(
+                        out=pt[:, j, :], in_=xa[:, l, j, :].bitcast(F32)[:, P * u : P * u + P], identity=ident[:]
+                    )
+                ptv = pt[:].rearrange("p j r -> p (j r)").bitcast(BF16).rearrange("p (c e) -> p c e", e=2)
+                for e in range(2):
+                    nc.scalar.activation(
+                        out=planes[:, 2 * u + e, :],
+                        in_=ptv[:, :, e],
+                        func=ACT.Identity,
+                        bias=bia[:, b, 2 * l + u, e : e + 1],
+                        scale=scl[:, b, l, u : u + 1],
+                    )
+            grp = gpool.tile([P, J * P, 4], BF16, align_bytes=64, name="grp")
+            if (b, l) in V_INTERLEAVE:
+                interleave(nc.vector.tensor_copy, grp[:], planes[:])
+            else:
+                interleave(nc.scalar.copy, grp[:], planes[:])
+            return grp
 
-            acc = opool.tile([P, J, DM], F32)
+        def quant(b, l, grp):
+            ac = cpool.tile([P, J * P], U32, align_bytes=64, name="ac")
+            asc = cpool.tile([P, J * P], U8, align_bytes=64, name="asc")
+            nc.vector.quantize_mx(out=ac[:].bitcast(FP8X4), scales=asc[:], in_=grp[:].rearrange("p c t -> p (c t)"))
+            codes[(b, l)] = (ac, asc)
+
+        def stt(b, m):
+            if m == 0:
+                acc = opool.tile([P, J, DM], F32, name="acc")
+                accs[b] = acc
+                other = cbc[:, b, :].unsqueeze(1).to_broadcast([P, J, DM])
+            else:
+                acc = accs[b]
+                other = acc[:]
             nc.vector.scalar_tensor_tensor(
                 out=acc[:],
-                in0=xm[:, 0],
-                scalar=mmf[:, M * b : M * b + 1],
-                in1=cbc[:, b, :].unsqueeze(1).to_broadcast([P, J, DM]),
+                in0=xms[b][:, m],
+                scalar=mmf[:, M * b + m : M * b + m + 1],
+                in1=other,
                 op0=ALU.mult,
                 op1=ALU.add,
             )
-            for m in range(1, M):
-                nc.vector.scalar_tensor_tensor(
-                    out=acc[:],
-                    in0=xm[:, m],
-                    scalar=mmf[:, M * b + m : M * b + m + 1],
-                    in1=acc[:],
-                    op0=ALU.mult,
-                    op1=ALU.add,
-                )
+
+        def mx(b, fine_store):
+            acc = accs[b]
+            dst = out[b, 1:POS, :].rearrange("(p j) n -> p j n", j=J)
+            pos = []
             for j in range(J):
-                po = psO.tile([P, DM], F32)
+                po = psO.tile([P, DM], F32, name="po")
+                pos.append(po)
                 for l in range(L):
-                    ac, asc = codes[l]
+                    ac, asc = codes[(b, l)]
                     nc.tensor.matmul_mx(
                         out=po[:],
                         lhsT=ac[:, P * j : P * j + P].bitcast(FP8X4),
@@ -197,7 +226,43 @@ def tile_edgepruner_t_kernel(
                         start=(l == 0),
                         stop=(l == L - 1),
                     )
-                nc.vector.tensor_tensor(out=acc[:, j, :], in0=acc[:, j, :], in1=po[:], op=ALU.add)
-            nc.sync.dma_start(
-                out=out[b, 1:POS, :].rearrange("(p j) n -> p (j n)", j=J), in_=acc[:].rearrange("p j n -> p (j n)")
-            )
+            for j in range(J):
+                nc.vector.tensor_tensor(out=acc[:, j, :], in0=acc[:, j, :], in1=pos[j][:], op=ALU.add)
+                if fine_store and j % 2 == 1:
+                    nc.sync.dma_start(out=dst[:, j - 1 : j + 1, :], in_=acc[:, j - 1 : j + 1, :])
+            if not fine_store:
+                nc.sync.dma_start(out=dst, in_=acc[:])
+
+        w_regroup(0, nc.vector.tensor_copy)
+        g00 = t1(0, 0)
+        w_regroup(1, nc.scalar.copy)
+        for b in range(B):
+            spread_const(b)
+        w_quant(0)
+        w_quant(1)
+        quant(0, 0, g00)
+        stt(0, 0)
+        g01 = t1(0, 1)
+        quant(0, 1, g01)
+        o8f = const.tile([B, DM], F32)
+        nc.vector.tensor_copy(out=o8f[:], in_=o8[:])
+        nc.scalar.dma_start(out=out[:, 0, :], in_=o8f[:])
+
+        ahead = min(4, 4)
+        for b in range(B):
+            nxt = b + 1
+            if nxt < B:
+                ga = t1(nxt, 0)
+            if b > 0:
+                stt(b, 0)
+            if nxt < B:
+                quant(nxt, 0, ga)
+                gb = t1(nxt, 1)
+            stt(b, 1)
+            stt(b, 2)
+            if nxt < B:
+                quant(nxt, 1, gb)
+            if b + ahead < B:
+                issue(load_attn(b + ahead, False))
+                issue(load_mlp(b + ahead, False))
+            mx(b, b == B - 1)

from contextlib import ExitStack

import concourse.mybir as mybir
from concourse.masks import make_identity

F32 = mybir.dt.float32
BF16 = mybir.dt.bfloat16
U32 = mybir.dt.uint32
U8 = mybir.dt.uint8
FP8X4 = mybir.dt.float8_e4m3fn_x4
ALU = mybir.AluOpType
ACT = mybir.ActivationFunctionType

L, B, POS, H, DH, DM = 2, 8, 513, 8, 64, 512
M = 3
P = 128
J = 4
R = POS - 1
KL = H * DH

FLOPS = 2 * B * R * L * KL * DM
BYTES = 2 * (L * B * R * KL + M * B * R * DM + L * KL * DM) + 4 * B * POS * DM

PIN = False
V_INTERLEAVE = ()


def interleave(eng_copy, dst, src):
    eng_copy(
        out=dst.rearrange("p (c i) t -> p c t i", i=4),
        in_=src.rearrange("p t (c i) -> p c t i", i=4),
    )


def tile_edgepruner_t_kernel(
    tc, attn_cache, mlp_cache, mlp_mask, attn_mask, modal_attention, modal_mlp, W_O, post_bias, orig_in, out
):
    nc = tc.nc
    with ExitStack() as ctx:
        const = ctx.enter_context(tc.tile_pool(name="const", bufs=1))
        apool = ctx.enter_context(tc.tile_pool(name="apool", bufs=4))
        mpool = ctx.enter_context(tc.tile_pool(name="mpool", bufs=4))
        opool = ctx.enter_context(tc.tile_pool(name="opool", bufs=3))
        ppool = ctx.enter_context(tc.tile_pool(name="ppool", bufs=3))
        gpool = ctx.enter_context(tc.tile_pool(name="gpool", bufs=3))
        cpool = ctx.enter_context(tc.tile_pool(name="cpool", bufs=4))
        psT = ctx.enter_context(tc.psum_pool(name="psT", bufs=4))
        psO = ctx.enter_context(tc.psum_pool(name="psO", bufs=4))
        if PIN:
            ctx.enter_context(tc.manual_schedule())

        xas = {}
        xms = {}

        def load_attn(b, fine):
            xa = apool.tile([P, L, J, KL], BF16, name="xa")
            xas[b] = xa
            src = attn_cache[:, b, 1:POS, :, :].rearrange("l (p j) h d -> p l (j h d)", j=J)
            dst = xa[:].rearrange("p l j k -> p l (j k)")
            if fine:
                return [(dst[:, l, :], src[:, l, :]) for l in range(L)]
            return [(dst, src)]

        def load_mlp(b, fine):
            xm = mpool.tile([P, M, J, DM], BF16, name="xm")
            xms[b] = xm
            src = mlp_cache[:, b, 1:POS, :].rearrange("m (p j) n -> p m (j n)", j=J)
            dst = xm[:].rearrange("p m j n -> p m (j n)")
            if fine:
                return [(dst[:, m, :], src[:, m, :]) for m in range(M)]
            return [(dst, src)]

        def issue(pairs):
            for dst, src in pairs:
                nc.sync.dma_start(out=dst, in_=src)

        wraw = const.tile([P, 2 * L, 2, DM], BF16)
        wsrc = W_O.rearrange("l h d n -> (l h d) n").rearrange("(g p e) n -> p g (e n)", g=2 * L, p=P, e=2)
        wdst = wraw[:].rearrange("p g e n -> p g (e n)")
        a0 = load_attn(0, True)
        m0 = load_mlp(0, True)
        issue([(wdst[:, 0:2, :], wsrc[:, 0:2, :]), a0[0], (wdst[:, 2:4, :], wsrc[:, 2:4, :]), m0[0], a0[1], m0[1], m0[2]])

        am_bc = const.tile([P, B * L * H], BF16)
        nc.scalar.dma_start(out=am_bc[:], in_=attn_mask.rearrange("b l h -> (b l h)").partition_broadcast(P))
        modalT = const.tile([P, 2 * L, 2], BF16)
        with nc.allow_non_contiguous_dma(reason="512 four-byte pieces, once"):
            nc.scalar.dma_start(
                out=modalT[:],
                in_=modal_attention.rearrange("l h d -> (l h d)").rearrange("(g p e) -> p g e", g=2 * L, p=P, e=2),
            )
        mmr = const.tile([B, M], BF16)
        nc.scalar.dma_start(out=mmr[:], in_=mlp_mask)
        mod8 = const.tile([B, M, DM], BF16)
        nc.scalar.dma_start(
            out=mod8[:].rearrange("b m n -> b (m n)"), in_=modal_mlp.rearrange("m n -> (m n)").partition_broadcast(B)
        )
        pb8 = const.tile([B, L, DM], BF16)
        nc.scalar.dma_start(
            out=pb8[:].rearrange("b l n -> b (l n)"), in_=post_bias.rearrange("l n -> (l n)").partition_broadcast(B)
        )
        mm_bc = const.tile([P, B * M], BF16)
        nc.scalar.dma_start(out=mm_bc[:], in_=mlp_mask.rearrange("b m -> (b m)").partition_broadcast(P))
        o8 = const.tile([B, DM], BF16)
        nc.scalar.dma_start(out=o8[:], in_=orig_in[:, 0, :])

        ident = const.tile([P, P], F32)
        make_identity(nc, ident[:])

        for b in range(1, min(4, 4)):
            issue(load_attn(b, False))
            issue(load_mlp(b, False))

        crow = const.tile([P, DM], F32)
        nc.vector.memset(crow[:], 0.0)
        scl = const.tile([P, B, L, 2], F32)
        amv = am_bc[:].rearrange("p (b l u g) -> p b l u g", b=B, l=L, u=2, g=4)
        for g in range(4):
            nc.vector.tensor_copy(out=scl[32 * g : 32 * g + 32], in_=amv[32 * g : 32 * g + 32, :, :, :, g])
        om = const.tile([P, B * L * 2], F32)
        nc.vector.tensor_scalar(
            out=om[:], in0=scl[:].rearrange("p b l u -> p (b l u)"), scalar1=-1.0, scalar2=1.0, op0=ALU.mult, op1=ALU.add
        )
        bia = const.tile([P, B, 2 * L, 2], F32)
        nc.vector.tensor_tensor(
            out=bia[:],
            in0=om[:].rearrange("p (b g) -> p b g", g=2 * L).unsqueeze(3).to_broadcast([P, B, 2 * L, 2]),
            in1=modalT[:].unsqueeze(1).to_broadcast([P, B, 2 * L, 2]),
            op=ALU.mult,
        )
        omr = const.tile([B, M], F32)
        nc.vector.tensor_scalar(out=omr[:], in0=mmr[:], scalar1=-1.0, scalar2=1.0, op0=ALU.mult, op1=ALU.add)
        nc.vector.tensor_tensor(out=crow[0:B, :], in0=pb8[:, 0, :], in1=pb8[:, 1, :], op=ALU.add)
        for m in range(M):
            nc.vector.scalar_tensor_tensor(
                out=crow[0:B, :], in0=mod8[:, m, :], scalar=omr[:, m : m + 1], in1=crow[0:B, :], op0=ALU.mult, op1=ALU.add
            )
        mmf = const.tile([P, B * M], F32)
        nc.vector.tensor_copy(out=mmf[:], in_=mm_bc[:])

        cbc = const.tile([P, B, DM], F32)

        def spread_const(b):
            po = psO.tile([P, DM], F32, name="po")
            nc.tensor.matmul(out=po[:], lhsT=ident[:, b : b + 1].to_broadcast([P, P]), rhs=crow[:], start=True, stop=True)
            nc.scalar.copy(out=cbc[:, b, :], in_=po[:])

        wg = const.tile([P, L, DM, 4], BF16, align_bytes=64)
        wc = const.tile([P, L, DM], U32, align_bytes=64)
        ws = const.tile([P, L, DM], U8, align_bytes=64)

        def w_regroup(l, eng_copy):
            interleave(eng_copy, wg[:, l], wraw[:, 2 * l : 2 * l + 2].rearrange("p u e n -> p (u e) n"))

        def w_quant(l):
            nc.vector.quantize_mx(
                out=wc[:, l, :].bitcast(FP8X4), scales=ws[:, l, :], in_=wg[:, l].rearrange("p n t -> p (n t)")
            )

        codes = {}
        accs = {}

        def t1(b, l):
            xa = xas[b]
            planes = ppool.tile([P, 4, J * P], BF16, name="planes")
            for u in range(2):
                pt = psT.tile([P, J, P], F32, name="pt")
                for j in range(J):
                    nc.tensor.transpose(
                        out=pt[:, j, :], in_=xa[:, l, j, :].bitcast(F32)[:, P * u : P * u + P], identity=ident[:]
                    )
                ptv = pt[:].rearrange("p j r -> p (j r)").bitcast(BF16).rearrange("p (c e) -> p c e", e=2)
                for e in range(2):
                    nc.scalar.activation(
                        out=planes[:, 2 * u + e, :],
                        in_=ptv[:, :, e],
                        func=ACT.Identity,
                        bias=bia[:, b, 2 * l + u, e : e + 1],
                        scale=scl[:, b, l, u : u + 1],
                    )
            grp = gpool.tile([P, J * P, 4], BF16, align_bytes=64, name="grp")
            if (b, l) in V_INTERLEAVE:
                interleave(nc.vector.tensor_copy, grp[:], planes[:])
            else:
                interleave(nc.scalar.copy, grp[:], planes[:])
            return grp

        def quant(b, l, grp):
            ac = cpool.tile([P, J * P], U32, align_bytes=64, name="ac")
            asc = cpool.tile([P, J * P], U8, align_bytes=64, name="asc")
            nc.vector.quantize_mx(out=ac[:].bitcast(FP8X4), scales=asc[:], in_=grp[:].rearrange("p c t -> p (c t)"))
            codes[(b, l)] = (ac, asc)

        def stt(b, m):
            if m == 0:
                acc = opool.tile([P, J, DM], F32, name="acc")
                accs[b] = acc
                other = cbc[:, b, :].unsqueeze(1).to_broadcast([P, J, DM])
            else:
                acc = accs[b]
                other = acc[:]
            nc.vector.scalar_tensor_tensor(
                out=acc[:],
                in0=xms[b][:, m],
                scalar=mmf[:, M * b + m : M * b + m + 1],
                in1=other,
                op0=ALU.mult,
                op1=ALU.add,
            )

        def mx(b, fine_store):
            acc = accs[b]
            dst = out[b, 1:POS, :].rearrange("(p j) n -> p j n", j=J)
            pos = []
            for j in range(J):
                po = psO.tile([P, DM], F32, name="po")
                pos.append(po)
                for l in range(L):
                    ac, asc = codes[(b, l)]
                    nc.tensor.matmul_mx(
                        out=po[:],
                        lhsT=ac[:, P * j : P * j + P].bitcast(FP8X4),
                        lhsT_scale=asc[:, P * j : P * j + P],
                        rhs=wc[:, l, :].bitcast(FP8X4),
                        rhs_scale=ws[:, l, :],
                        start=(l == 0),
                        stop=(l == L - 1),
                    )
            for j in range(J):
                nc.vector.tensor_tensor(out=acc[:, j, :], in0=acc[:, j, :], in1=pos[j][:], op=ALU.add)
                if fine_store and j % 2 == 1:
                    nc.sync.dma_start(out=dst[:, j - 1 : j + 1, :], in_=acc[:, j - 1 : j + 1, :])
            if not fine_store:
                nc.sync.dma_start(out=dst, in_=acc[:])

        w_regroup(0, nc.vector.tensor_copy)
        g00 = t1(0, 0)
        w_regroup(1, nc.scalar.copy)
        for b in range(B):
            spread_const(b)
        w_quant(0)
        w_quant(1)
        quant(0, 0, g00)
        stt(0, 0)
        g01 = t1(0, 1)
        quant(0, 1, g01)
        o8f = const.tile([B, DM], F32)
        nc.vector.tensor_copy(out=o8f[:], in_=o8[:])
        nc.scalar.dma_start(out=out[:, 0, :], in_=o8f[:])

        ahead = min(4, 4)
        for b in range(B):
            nxt = b + 1
            if nxt < B:
                ga = t1(nxt, 0)
            if b > 0:
                stt(b, 0)
            if nxt < B:
                quant(nxt, 0, ga)
                gb = t1(nxt, 1)
            stt(b, 1)
            stt(b, 2)
            if nxt < B:
                quant(nxt, 1, gb)
            if b + ahead < B:
                issue(load_attn(b + ahead, False))
                issue(load_mlp(b + ahead, False))
            mx(b, b == B - 1)
